import numpy as np
import ml_dtypes


def mxq(x, axis, fmt="e4m3"):
    dtype, down = {"e4m3": (ml_dtypes.float8_e4m3fn, 7), "e5m2": (ml_dtypes.float8_e5m2, 14)}[fmt]
    v = np.moveaxis(np.asarray(x, np.float32).astype(ml_dtypes.bfloat16).astype(np.float64), axis, -1)
    blocks = v.reshape(v.shape[:-1] + (-1, 32))
    amax = np.abs(blocks).max(-1, keepdims=True)
    byte = np.maximum(np.where(amax > 0, np.frexp(amax)[1] - 1 + 127, 0) - down, 1)
    scale = np.exp2(byte - 127.0)
    codes = (blocks / scale).astype(np.float32).astype(dtype).astype(np.float64)
    return np.moveaxis((codes * scale).reshape(v.shape), -1, axis)


WIDE = False


def mx_kscale(k):
    if not WIDE:
        return np.ones(k)
    levels = np.array([10, -10, 5, -5, 0])
    if k % 512:
        return np.exp2(np.random.permutation(np.resize(levels, k // 32))).repeat(32)
    a = np.empty((k // 512, 16))
    for p in range(k // 512):
        a[p, :8] = np.random.permutation(np.resize(levels, 8))
        for g in range(8):
            far = levels[np.abs(levels - a[p, g]) >= 10]
            a[p, g + 8] = far[np.random.randint(len(far))]
    return np.exp2(a.ravel()).repeat(32)


BF16 = ml_dtypes.bfloat16


def bf(x):
    return np.asarray(x, np.float32).astype(BF16)


def f64(x):
    return np.asarray(x).astype(np.float64)


B, S, SV, H, DH = 1, 1024, 1024, 8, 64
SCALE = DH ** (-0.5)


def _flatten_like_module(t):
    b, s, h, dh = t.shape
    return np.transpose(t, (0, 2, 1, 3)).reshape(b, s, h * dh)


def _heads_to_batch(t):
    b, s, d = t.shape
    t = t.reshape(b, s, H, d // H)
    t = np.transpose(t, (0, 2, 1, 3))
    return t.reshape(b * H, s, d // H)


def setup_inputs():
    a = np.sqrt(2.0 / (SCALE * np.sqrt(S)))
    sc = mx_kscale(S)
    f = np.repeat(sc.reshape(H, S // H).T, H, axis=0)[None, :, :, None]
    return {"query": bf(np.random.standard_normal((B, S, H, DH)) * a * f),
            "key": bf(np.random.standard_normal((B, S, H, DH)) * a / f),
            "value": bf(np.random.standard_normal((B, SV, H, DH)))}


def reference(query, key, value):
    q = _heads_to_batch(_flatten_like_module(f64(query)))
    k = _heads_to_batch(_flatten_like_module(f64(key)))
    scores = (mxq(q, 1, "e4m3").transpose(0, 2, 1) @ mxq(k, 1, "e4m3")) * SCALE
    e = np.exp(scores - scores.max(axis=2, keepdims=True))
    return e / e.sum(axis=2, keepdims=True)

@@ -1,0 +1,166 @@
+from contextlib import ExitStack
+
+import concourse.mybir as mybir
+
+BF16 = mybir.dt.bfloat16
+F32 = mybir.dt.float32
+U32 = mybir.dt.uint32
+U8 = mybir.dt.uint8
+FP8X4 = mybir.dt.float8_e4m3fn_x4
+ALU = mybir.AluOpType
+ACT = mybir.ActivationFunctionType
+
+P = 128
+PACK = 4
+SEQ, HEADS, DH = 1024, 8, 64
+MATS = SEQ // P
+QUAD = 32
+QUADS = P // QUAD
+PASSES = HEADS // QUADS
+DUO = 2
+PAIRS = MATS // DUO
+COLS = DUO * DH
+RUN = 4
+SCALE = DH ** -0.5
+
+FLOPS = 2 * MATS * DH * DH * SEQ
+BYTES = 2 * SEQ * HEADS * DH * 2 + MATS * DH * DH * 4
+
+
+def regroup(copy, raw, grouped):
+    copy(
+        out=grouped.rearrange("p a (e i) t -> p a e t i", i=RUN),
+        in_=raw.rearrange("p t a (e i) -> p a e t i", i=RUN),
+    )
+
+
+def tile_flaxattention2_s_kernel(tc, query, key, value, out):
+    nc = tc.nc
+    q_view = query.rearrange("b (m t g) (q c) d -> q (b m) (t g) (c d)", t=PACK, g=MATS, c=PASSES)
+    k_view = key.rearrange("b (m t g) (q c) d -> q (b m) (t g) (c d)", t=PACK, g=MATS, c=PASSES)
+    out_view = out.rearrange("(pair a) d e -> (a d) pair e", a=DUO)
+
+    with ExitStack() as ctx:
+        ctx.enter_context(tc.manual_schedule())
+        loads = ctx.enter_context(tc.tile_pool(name="loads", bufs=1))
+        operands = ctx.enter_context(tc.tile_pool(name="operands", bufs=PAIRS))
+        soft = ctx.enter_context(tc.tile_pool(name="soft", bufs=1))
+        psum = ctx.enter_context(tc.psum_pool(name="psum", bufs=PAIRS))
+
+        k_raw = loads.tile([P, PACK, MATS, PASSES, DH], BF16)
+        q_raw = loads.tile([P, PACK, MATS, PASSES, DH], BF16)
+        for raw, view in ((k_raw, k_view), (q_raw, q_view)):
+            for q in (0, 2, 1, 3):
+                quadrant = slice(q * QUAD, (q + 1) * QUAD)
+                nc.sync.dma_start(out=raw[quadrant].rearrange("m t g c d -> m (t g) (c d)"), in_=view[q])
+
+        warm = soft.tile([P, 1], F32)
+        nc.vector.memset(warm[:], 0.0)
+        nc.scalar.activation(out=warm[:], in_=warm[:], func=ACT.Exp)
+
+        def regroup_both_passes(raw, pair, grouped):
+            mats = slice(pair * DUO, (pair + 1) * DUO)
+            regroup(nc.scalar.copy, raw[:, :, mats, 0], grouped[:, 0])
+            regroup(nc.vector.tensor_copy, raw[:, :, mats, 1], grouped[:, 1])
+
+
+        k_grouped_tiles = []
+        q_grouped_tiles = []
+        k_code_tiles = []
+        k_scale_tiles = []
+        score_tiles = []
+
+        def regroup_k(pair):
+            k_grouped = operands.tile([P, PASSES, DUO, DH, PACK], BF16, align_bytes=64)
+            regroup_both_passes(k_raw, pair, k_grouped)
+            k_grouped_tiles.append(k_grouped)
+
+        def regroup_q(pair):
+            q_grouped = operands.tile([P, PASSES, DUO, DH, PACK], BF16, align_bytes=64)
+            regroup_both_passes(q_raw, pair, q_grouped)
+            q_grouped_tiles.append(q_grouped)
+
+        def quantise_k(pair):
+            k_codes = operands.tile([P, PASSES * COLS], U32, align_bytes=64)
+            k_scales = operands.tile([P, PASSES * COLS], U8, align_bytes=64)
+            nc.vector.quantize_mx(
+                out=k_codes[:].bitcast(FP8X4),
+                scales=k_scales[:],
+                in_=k_grouped_tiles[pair][:].rearrange("p c a d t -> p (c a d t)"),
+            )
+            k_code_tiles.append(k_codes)
+            k_scale_tiles.append(k_scales)
+
+        def quantise_q_and_multiply(pair):
+            q_codes = operands.tile([P, PASSES * COLS], U32, align_bytes=64)
+            q_scales = operands.tile([P, PASSES * COLS], U8, align_bytes=64)
+            scores = psum.tile([P, COLS], F32)
+            score_tiles.append(scores)
+            for c in range(PASSES):
+                cols = slice(c * COLS, (c + 1) * COLS)
+                nc.vector.quantize_mx(
+                    out=q_codes[:, cols].bitcast(FP8X4),
+                    scales=q_scales[:, cols],
+                    in_=q_grouped_tiles[pair][:, c].rearrange("p a d t -> p (a d t)"),
+                )
+                nc.tensor.matmul_mx(
+                    out=scores[:],
+                    lhsT=q_codes[:, cols].bitcast(FP8X4),
+                    lhsT_scale=q_scales[:, cols],
+                    rhs=k_code_tiles[pair][:, cols].bitcast(FP8X4),
+                    rhs_scale=k_scale_tiles[pair][:, cols],
+                    start=(c == 0),
+                    stop=(c == PASSES - 1),
+                )
+
+        for pair in range(PAIRS):
+            regroup_k(pair)
+            if pair > 0:
+                quantise_q_and_multiply(pair - 1)
+            regroup_q(pair)
+            quantise_k(pair)
+        quantise_q_and_multiply(PAIRS - 1)
+
+        flipped = soft.tile([P, PAIRS, DH], F32)
+        shift = soft.tile([P, PAIRS], F32)
+        grown = soft.tile([P, PAIRS, DH], F32)
+        row_sum = soft.tile([P, PAIRS], F32)
+        inverse = soft.tile([P, PAIRS], F32)
+        probs = soft.tile([P, PAIRS, DH], F32)
+
+        for pair in range(PAIRS):
+            one = slice(pair, pair + 1)
+            for a in range(DUO):
+                half = slice(a * DH, (a + 1) * DH)
+                nc.vector.tensor_scalar(
+                    out=flipped[half, pair, :],
+                    in0=score_tiles[pair][half, half],
+                    scalar1=-SCALE,
+                    scalar2=None,
+                    op0=ALU.mult,
+                    op1=ALU.min,
+                    accum_out=shift[half, one],
+                )
+            nc.scalar.activation(
+                out=grown[:, pair, :],
+                in_=flipped[:, pair, :],
+                func=ACT.Exp,
+                bias=shift[:, one],
+                scale=-1.0,
+                accum_out=row_sum[:, one],
+            )
+
+        for group in (range(PAIRS - 1), range(PAIRS - 1, PAIRS)):
+            for pair in group:
+                one = slice(pair, pair + 1)
+                nc.vector.reciprocal(out=inverse[:, one], in_=row_sum[:, one])
+            for pair in group:
+                one = slice(pair, pair + 1)
+                nc.vector.tensor_scalar(
+                    out=probs[:, pair, :],
+                    in0=grown[:, pair, :],
+                    scalar1=inverse[:, one],
+                    scalar2=None,
+                    op0=ALU.mult,
+                )
+                nc.sync.dma_start(out=out_view[:, pair, :], in_=probs[:, pair, :])

@@ -50,9 +50,9 @@ def tile_flaxattention2_s_kernel(tc, query, key, value, out):
         k_raw = loads.tile([P, PACK, MATS, PASSES, DH], BF16)
         q_raw = loads.tile([P, PACK, MATS, PASSES, DH], BF16)
         for raw, view in ((k_raw, k_view), (q_raw, q_view)):
-            for q in (0, 2, 1, 3):
+            for q, queue in ((0, nc.sync), (2, nc.scalar), (1, nc.sync), (3, nc.scalar)):
                 quadrant = slice(q * QUAD, (q + 1) * QUAD)
-                nc.sync.dma_start(out=raw[quadrant].rearrange("m t g c d -> m (t g) (c d)"), in_=view[q])
+                queue.dma_start(out=raw[quadrant].rearrange("m t g c d -> m (t g) (c d)"), in_=view[q])
 
         warm = soft.tile([P, 1], F32)
         nc.vector.memset(warm[:], 0.0)

@@ -27,114 +27,103 @@ FLOPS = 2 * MATS * DH * DH * SEQ
 BYTES = 2 * SEQ * HEADS * DH * 2 + MATS * DH * DH * 4
 
 
-def regroup(copy, raw, grouped):
+def regroup(copy, raw, grouped, c):
     copy(
-        out=grouped.rearrange("p a (e i) t -> p a e t i", i=RUN),
-        in_=raw.rearrange("p t a (e i) -> p a e t i", i=RUN),
+        out=grouped[:, c].rearrange("p a (e i) t -> p a e t i", i=RUN),
+        in_=raw.rearrange("p (t a) (c d) -> p t a c d", a=DUO, c=PASSES)[:, :, :, c].rearrange(
+            "p t a (e i) -> p a e t i", i=RUN
+        ),
     )
 
 
 def tile_flaxattention2_s_kernel(tc, query, key, value, out):
     nc = tc.nc
-    q_view = query.rearrange("b (m t g) (q c) d -> q (b m) (t g) (c d)", t=PACK, g=MATS, c=PASSES)
-    k_view = key.rearrange("b (m t g) (q c) d -> q (b m) (t g) (c d)", t=PACK, g=MATS, c=PASSES)
-    out_view = out.rearrange("(pair a) d e -> (a d) pair e", a=DUO)
+    view = "b (m t a pair) (q c) d -> pair q (b m) (t a) (c d)"
+    q_view = query.rearrange(view, t=PACK, a=DUO, pair=PAIRS, c=PASSES)
+    k_view = key.rearrange(view, t=PACK, a=DUO, pair=PAIRS, c=PASSES)
+    out_view = out.rearrange("(a pair) d e -> pair a d e", a=DUO)
 
     with ExitStack() as ctx:
         ctx.enter_context(tc.manual_schedule())
-        loads = ctx.enter_context(tc.tile_pool(name="loads", bufs=1))
+        keep = ctx.enter_context(tc.tile_pool(name="keep", bufs=1))
         operands = ctx.enter_context(tc.tile_pool(name="operands", bufs=PAIRS))
-        soft = ctx.enter_context(tc.tile_pool(name="soft", bufs=1))
         psum = ctx.enter_context(tc.psum_pool(name="psum", bufs=PAIRS))
 
-        k_raw = loads.tile([P, PACK, MATS, PASSES, DH], BF16)
-        q_raw = loads.tile([P, PACK, MATS, PASSES, DH], BF16)
-        for raw, view in ((k_raw, k_view), (q_raw, q_view)):
-            for q, queue in ((0, nc.sync), (2, nc.scalar), (1, nc.sync), (3, nc.scalar)):
-                quadrant = slice(q * QUAD, (q + 1) * QUAD)
-                queue.dma_start(out=raw[quadrant].rearrange("m t g c d -> m (t g) (c d)"), in_=view[q])
+        k_raw_tiles = []
+        q_raw_tiles = []
 
-        warm = soft.tile([P, 1], F32)
+        def load(raw, view):
+            for q in (0, 2, 1, 3):
+                nc.sync.dma_start(out=raw[q * QUAD : (q + 1) * QUAD], in_=view[q])
+
+        for pair in range(PAIRS):
+            k_raw = operands.tile([P, PACK * DUO, PASSES * DH], BF16)
+            load(k_raw, k_view[pair])
+            k_raw_tiles.append(k_raw)
+            q_raw = operands.tile([P, PACK * DUO, PASSES * DH], BF16)
+            load(q_raw, q_view[pair])
+            q_raw_tiles.append(q_raw)
+
+        warm = keep.tile([P, 1], F32)
         nc.vector.memset(warm[:], 0.0)
         nc.scalar.activation(out=warm[:], in_=warm[:], func=ACT.Exp)
 
-        def regroup_both_passes(raw, pair, grouped):
-            mats = slice(pair * DUO, (pair + 1) * DUO)
-            regroup(nc.scalar.copy, raw[:, :, mats, 0], grouped[:, 0])
-            regroup(nc.vector.tensor_copy, raw[:, :, mats, 1], grouped[:, 1])
+        def regroup_both_passes(raw, grouped):
+            regroup(nc.scalar.copy, raw[:], grouped, 0)
+            regroup(nc.vector.tensor_copy, raw[:], grouped, 1)
 
+        def quantise(grouped, codes, scales, first, passes):
+            cols = slice(first * COLS, (first + passes) * COLS)
+            nc.vector.quantize_mx(
+                out=codes[:, cols].bitcast(FP8X4),
+                scales=scales[:, cols],
+                in_=grouped[:, first : first + passes].rearrange("p c a d t -> p (c a d t)"),
+            )
 
-        k_grouped_tiles = []
-        q_grouped_tiles = []
-        k_code_tiles = []
-        k_scale_tiles = []
-        score_tiles = []
-
-        def regroup_k(pair):
+        def make_k(pair, between):
             k_grouped = operands.tile([P, PASSES, DUO, DH, PACK], BF16, align_bytes=64)
-            regroup_both_passes(k_raw, pair, k_grouped)
-            k_grouped_tiles.append(k_grouped)
-
-        def regroup_q(pair):
-            q_grouped = operands.tile([P, PASSES, DUO, DH, PACK], BF16, align_bytes=64)
-            regroup_both_passes(q_raw, pair, q_grouped)
-            q_grouped_tiles.append(q_grouped)
-
-        def quantise_k(pair):
+            regroup_both_passes(k_raw_tiles[pair], k_grouped)
+            between()
             k_codes = operands.tile([P, PASSES * COLS], U32, align_bytes=64)
             k_scales = operands.tile([P, PASSES * COLS], U8, align_bytes=64)
-            nc.vector.quantize_mx(
-                out=k_codes[:].bitcast(FP8X4),
-                scales=k_scales[:],
-                in_=k_grouped_tiles[pair][:].rearrange("p c a d t -> p (c a d t)"),
-            )
-            k_code_tiles.append(k_codes)
-            k_scale_tiles.append(k_scales)
+            quantise(k_grouped, k_codes, k_scales, 0, PASSES)
+            return k_codes, k_scales
 
-        def quantise_q_and_multiply(pair):
+        def make_scores(pair, k_codes, k_scales, between):
+            q_grouped = operands.tile([P, PASSES, DUO, DH, PACK], BF16, align_bytes=64)
+            regroup_both_passes(q_raw_tiles[pair], q_grouped)
+            between()
             q_codes = operands.tile([P, PASSES * COLS], U32, align_bytes=64)
             q_scales = operands.tile([P, PASSES * COLS], U8, align_bytes=64)
             scores = psum.tile([P, COLS], F32)
-            score_tiles.append(scores)
-            for c in range(PASSES):
+            for c in (1, 0):
                 cols = slice(c * COLS, (c + 1) * COLS)
-                nc.vector.quantize_mx(
-                    out=q_codes[:, cols].bitcast(FP8X4),
-                    scales=q_scales[:, cols],
-                    in_=q_grouped_tiles[pair][:, c].rearrange("p a d t -> p (a d t)"),
-                )
+                quantise(q_grouped, q_codes, q_scales, c, 1)
                 nc.tensor.matmul_mx(
                     out=scores[:],
                     lhsT=q_codes[:, cols].bitcast(FP8X4),
                     lhsT_scale=q_scales[:, cols],
-                    rhs=k_code_tiles[pair][:, cols].bitcast(FP8X4),
-                    rhs_scale=k_scale_tiles[pair][:, cols],
-                    start=(c == 0),
-                    stop=(c == PASSES - 1),
+                    rhs=k_codes[:, cols].bitcast(FP8X4),
+                    rhs_scale=k_scales[:, cols],
+                    start=(c == 1),
+                    stop=(c == 0),
                 )
+            return scores
 
-        for pair in range(PAIRS):
-            regroup_k(pair)
-            if pair > 0:
-                quantise_q_and_multiply(pair - 1)
-            regroup_q(pair)
-            quantise_k(pair)
-        quantise_q_and_multiply(PAIRS - 1)
+        flipped = keep.tile([P, PAIRS, DH], F32)
+        shift = keep.tile([P, PAIRS], F32)
+        grown = keep.tile([P, PAIRS, DH], F32)
+        row_sum = keep.tile([P, PAIRS], F32)
+        inverse = keep.tile([P, PAIRS], F32)
+        probs = keep.tile([P, PAIRS, DH], F32)
 
-        flipped = soft.tile([P, PAIRS, DH], F32)
-        shift = soft.tile([P, PAIRS], F32)
-        grown = soft.tile([P, PAIRS, DH], F32)
-        row_sum = soft.tile([P, PAIRS], F32)
-        inverse = soft.tile([P, PAIRS], F32)
-        probs = soft.tile([P, PAIRS, DH], F32)
-
-        for pair in range(PAIRS):
+        def exponentials(pair, scores):
             one = slice(pair, pair + 1)
             for a in range(DUO):
                 half = slice(a * DH, (a + 1) * DH)
                 nc.vector.tensor_scalar(
                     out=flipped[half, pair, :],
-                    in0=score_tiles[pair][half, half],
+                    in0=scores[half, half],
                     scalar1=-SCALE,
                     scalar2=None,
                     op0=ALU.mult,
@@ -150,17 +139,31 @@ def tile_flaxattention2_s_kernel(tc, query, key, value, out):
                 accum_out=row_sum[:, one],
             )
 
-        for group in (range(PAIRS - 1), range(PAIRS - 1, PAIRS)):
-            for pair in group:
-                one = slice(pair, pair + 1)
-                nc.vector.reciprocal(out=inverse[:, one], in_=row_sum[:, one])
-            for pair in group:
-                one = slice(pair, pair + 1)
-                nc.vector.tensor_scalar(
-                    out=probs[:, pair, :],
-                    in0=grown[:, pair, :],
-                    scalar1=inverse[:, one],
-                    scalar2=None,
-                    op0=ALU.mult,
-                )
-                nc.sync.dma_start(out=out_view[:, pair, :], in_=probs[:, pair, :])
+        def divide_and_store(pair, queues):
+            one = slice(pair, pair + 1)
+            nc.vector.reciprocal(out=inverse[:, one], in_=row_sum[:, one])
+            nc.vector.tensor_scalar(
+                out=probs[:, pair, :],
+                in0=grown[:, pair, :],
+                scalar1=inverse[:, one],
+                scalar2=None,
+                op0=ALU.mult,
+            )
+            for a, queue in enumerate(queues):
+                queue.dma_start(out=out_view[pair, a], in_=probs[a * DH : (a + 1) * DH, pair, :])
+
+        score_tiles = []
+
+        def first_half(pair):
+            if pair >= 0:
+                exponentials(pair, score_tiles[pair])
+
+        def second_half(pair):
+            if pair >= 0:
+                divide_and_store(pair, (nc.sync, nc.sync))
+
+        for pair in range(PAIRS):
+            k_codes, k_scales = make_k(pair, lambda: first_half(pair - 1))
+            score_tiles.append(make_scores(pair, k_codes, k_scales, lambda: second_half(pair - 1)))
+        exponentials(PAIRS - 1, score_tiles[PAIRS - 1])
+        divide_and_store(PAIRS - 1, (nc.sync, nc.scalar))

@@ -1,6 +1,7 @@
 from contextlib import ExitStack
 
 import concourse.mybir as mybir
+from concourse.masks import make_identity
 
 BF16 = mybir.dt.bfloat16
 F32 = mybir.dt.float32
@@ -19,6 +20,9 @@ QUADS = P // QUAD
 PASSES = HEADS // QUADS
 DUO = 2
 PAIRS = MATS // DUO
+LONG_PAIRS = 1
+MS = P // QUADS
+TPS = PACK // 2
 COLS = DUO * DH
 RUN = 4
 SCALE = DH ** -0.5
@@ -41,13 +45,14 @@ def tile_flaxattention2_s_kernel(tc, query, key, value, out):
     view = "b (m t a pair) (q c) d -> pair q (b m) (t a) (c d)"
     q_view = query.rearrange(view, t=PACK, a=DUO, pair=PAIRS, c=PASSES)
     k_view = key.rearrange(view, t=PACK, a=DUO, pair=PAIRS, c=PASSES)
+    k_long_view = key.rearrange("b (j a pair) h d -> pair (b j) a (h d)", a=DUO, pair=PAIRS)
     out_view = out.rearrange("(a pair) d e -> pair a d e", a=DUO)
 
     with ExitStack() as ctx:
         ctx.enter_context(tc.manual_schedule())
         keep = ctx.enter_context(tc.tile_pool(name="keep", bufs=1))
         operands = ctx.enter_context(tc.tile_pool(name="operands", bufs=PAIRS))
-        psum = ctx.enter_context(tc.psum_pool(name="psum", bufs=PAIRS))
+        psum = ctx.enter_context(tc.psum_pool(name="psum", bufs=2))
 
         k_raw_tiles = []
         q_raw_tiles = []
@@ -57,8 +62,12 @@ def tile_flaxattention2_s_kernel(tc, query, key, value, out):
                 nc.sync.dma_start(out=raw[q * QUAD : (q + 1) * QUAD], in_=view[q])
 
         for pair in range(PAIRS):
-            k_raw = operands.tile([P, PACK * DUO, PASSES * DH], BF16)
-            load(k_raw, k_view[pair])
+            if pair < LONG_PAIRS:
+                k_raw = keep.tile([P, DUO, HEADS * DH], BF16, name="k_long", bufs=LONG_PAIRS)
+                nc.sync.dma_start(out=k_raw[:], in_=k_long_view[pair])
+            else:
+                k_raw = keep.tile([P, PACK * DUO, PASSES * DH], BF16, name="k_raw", bufs=PAIRS - LONG_PAIRS)
+                load(k_raw, k_view[pair])
             k_raw_tiles.append(k_raw)
             q_raw = operands.tile([P, PACK * DUO, PASSES * DH], BF16)
             load(q_raw, q_view[pair])
@@ -67,6 +76,51 @@ def tile_flaxattention2_s_kernel(tc, query, key, value, out):
         warm = keep.tile([P, 1], F32)
         nc.vector.memset(warm[:], 0.0)
         nc.scalar.activation(out=warm[:], in_=warm[:], func=ACT.Exp)
+
+        ident_16 = keep.tile([P, P], BF16)
+        make_identity(nc, ident_16[:])
+        ident_32 = keep.tile([P, P], F32)
+        make_identity(nc, ident_32[:])
+
+        first_banks = []
+        word_tiles = []
+        second_banks = []
+        k_grouped_tiles = []
+        for pair in range(PAIRS):
+            k_grouped = operands.tile([P, PASSES, DUO, DH, PACK], BF16, align_bytes=64)
+            k_grouped_tiles.append(k_grouped)
+
+        def transpose_first(step):
+            pair, a = divmod(step, DUO)
+            bank = psum.tile([P, QUADS, P], BF16, name="first")
+            for q in range(QUADS):
+                nc.tensor.transpose(bank[:, q], k_raw_tiles[pair][:, a, q * P : (q + 1) * P], ident_16[:])
+            first_banks.append(bank)
+
+        def copy_first(step):
+            words = keep.tile([P, TPS, QUADS * MS], F32, name="words", bufs=LONG_PAIRS * DUO)
+            nc.scalar.copy(
+                out=words[:],
+                in_=first_banks[step][:]
+                .rearrange("p q j -> p (q j)")
+                .bitcast(F32)
+                .rearrange("p (y s) -> p s y", s=TPS),
+            )
+            word_tiles.append(words)
+
+        def transpose_second(step):
+            bank = psum.tile([P, TPS, P], F32, name="second")
+            for s in range(TPS):
+                nc.tensor.transpose(bank[:, s], word_tiles[step][:, s], ident_32[:])
+            second_banks.append(bank)
+
+        def copy_second(copy, step):
+            pair, a = divmod(step, DUO)
+            words = k_grouped_tiles[pair][:].rearrange("p c a d t -> p (c a d t)").bitcast(F32)
+            copy(
+                out=words.rearrange("p (c a d s) -> p c a d s", c=PASSES, a=DUO, s=TPS)[:, :, a],
+                in_=second_banks[step][:].rearrange("p s (c d) -> p c d s", c=PASSES),
+            )
 
         def regroup_both_passes(raw, grouped):
             regroup(nc.scalar.copy, raw[:], grouped, 0)
@@ -80,35 +134,50 @@ def tile_flaxattention2_s_kernel(tc, query, key, value, out):
                 in_=grouped[:, first : first + passes].rearrange("p c a d t -> p (c a d t)"),
             )
 
-        def make_k(pair, between):
-            k_grouped = operands.tile([P, PASSES, DUO, DH, PACK], BF16, align_bytes=64)
-            regroup_both_passes(k_raw_tiles[pair], k_grouped)
-            between()
+        def regroup_k(pair):
+            regroup_both_passes(k_raw_tiles[pair], k_grouped_tiles[pair])
+
+        k_operands = {}
+
+        def quantise_k(pair):
             k_codes = operands.tile([P, PASSES * COLS], U32, align_bytes=64)
             k_scales = operands.tile([P, PASSES * COLS], U8, align_bytes=64)
-            quantise(k_grouped, k_codes, k_scales, 0, PASSES)
-            return k_codes, k_scales
+            quantise(k_grouped_tiles[pair], k_codes, k_scales, 0, PASSES)
+            k_operands[pair] = (k_codes, k_scales)
 
-        def make_scores(pair, k_codes, k_scales, between):
+        q_grouped_tiles = {}
+        q_operands = {}
+
+        def regroup_q(pair):
             q_grouped = operands.tile([P, PASSES, DUO, DH, PACK], BF16, align_bytes=64)
             regroup_both_passes(q_raw_tiles[pair], q_grouped)
-            between()
-            q_codes = operands.tile([P, PASSES * COLS], U32, align_bytes=64)
-            q_scales = operands.tile([P, PASSES * COLS], U8, align_bytes=64)
-            scores = psum.tile([P, COLS], F32)
-            for c in (1, 0):
-                cols = slice(c * COLS, (c + 1) * COLS)
-                quantise(q_grouped, q_codes, q_scales, c, 1)
-                nc.tensor.matmul_mx(
-                    out=scores[:],
-                    lhsT=q_codes[:, cols].bitcast(FP8X4),
-                    lhsT_scale=q_scales[:, cols],
-                    rhs=k_codes[:, cols].bitcast(FP8X4),
-                    rhs_scale=k_scales[:, cols],
-                    start=(c == 1),
-                    stop=(c == 0),
-                )
-            return scores
+            q_grouped_tiles[pair] = q_grouped
+
+        def quantise_q(pair, passes):
+            if pair not in q_operands:
+                q_codes = operands.tile([P, PASSES * COLS], U32, align_bytes=64)
+                q_scales = operands.tile([P, PASSES * COLS], U8, align_bytes=64)
+                q_operands[pair] = (q_codes, q_scales)
+            quantise(q_grouped_tiles[pair], *q_operands[pair], passes.start, len(passes))
+
+        score_tiles = {}
+
+        def multiply(pair, c, start):
+            if start:
+                scores = psum.tile([P, COLS], F32, bufs=PAIRS)
+                score_tiles[pair] = scores
+            q_codes, q_scales = q_operands[pair]
+            k_codes, k_scales = k_operands[pair]
+            cols = slice(c * COLS, (c + 1) * COLS)
+            nc.tensor.matmul_mx(
+                out=score_tiles[pair][:],
+                lhsT=q_codes[:, cols].bitcast(FP8X4),
+                lhsT_scale=q_scales[:, cols],
+                rhs=k_codes[:, cols].bitcast(FP8X4),
+                rhs_scale=k_scales[:, cols],
+                start=start,
+                stop=not start,
+            )
 
         flipped = keep.tile([P, PAIRS, DH], F32)
         shift = keep.tile([P, PAIRS], F32)
@@ -117,7 +186,8 @@ def tile_flaxattention2_s_kernel(tc, query, key, value, out):
         inverse = keep.tile([P, PAIRS], F32)
         probs = keep.tile([P, PAIRS, DH], F32)
 
-        def exponentials(pair, scores):
+        def exponentials(pair):
+            scores = score_tiles[pair]
             one = slice(pair, pair + 1)
             for a in range(DUO):
                 half = slice(a * DH, (a + 1) * DH)
@@ -152,18 +222,44 @@ def tile_flaxattention2_s_kernel(tc, query, key, value, out):
             for a, queue in enumerate(queues):
                 queue.dma_start(out=out_view[pair, a], in_=probs[a * DH : (a + 1) * DH, pair, :])
 
-        score_tiles = []
+        transpose_first(0)
+        transpose_first(1)
+        copy_first(0)
+        copy_first(1)
+        transpose_second(0)
+        transpose_second(1)
+        regroup_q(0)
+        copy_second(nc.vector.tensor_copy, 0)
+        copy_second(nc.scalar.copy, 1)
+        regroup_k(1)
+        quantise_q(0, range(PASSES))
+        quantise_k(0)
+        multiply(0, 0, True)
+        multiply(0, 1, False)
 
-        def first_half(pair):
-            if pair >= 0:
-                exponentials(pair, score_tiles[pair])
-
-        def second_half(pair):
-            if pair >= 0:
-                divide_and_store(pair, (nc.sync, nc.sync))
-
-        for pair in range(PAIRS):
-            k_codes, k_scales = make_k(pair, lambda: first_half(pair - 1))
-            score_tiles.append(make_scores(pair, k_codes, k_scales, lambda: second_half(pair - 1)))
-        exponentials(PAIRS - 1, score_tiles[PAIRS - 1])
-        divide_and_store(PAIRS - 1, (nc.sync, nc.scalar))
+        quantise_k(1)
+        regroup_q(1)
+        exponentials(0)
+        quantise_q(1, range(PASSES))
+        multiply(1, 0, True)
+        multiply(1, 1, False)
+        regroup_k(2)
+        divide_and_store(0, (nc.sync, nc.sync))
+        quantise_k(2)
+        regroup_q(2)
+        exponentials(1)
+        quantise_q(2, range(PASSES))
+        multiply(2, 0, True)
+        multiply(2, 1, False)
+        regroup_k(3)
+        divide_and_store(1, (nc.sync, nc.sync))
+        quantise_k(3)
+        regroup_q(3)
+        exponentials(2)
+        quantise_q(3, range(1, 2))
+        multiply(3, 1, True)
+        quantise_q(3, range(0, 1))
+        multiply(3, 0, False)
+        divide_and_store(2, (nc.sync, nc.sync))
+        exponentials(3)
+        divide_and_store(3, (nc.sync, nc.scalar))

@@ -20,7 +20,7 @@ QUADS = P // QUAD
 PASSES = HEADS // QUADS
 DUO = 2
 PAIRS = MATS // DUO
-LONG_PAIRS = 1
+LONG_PAIRS = 3
 MS = P // QUADS
 TPS = PACK // 2
 COLS = DUO * DH
@@ -46,7 +46,7 @@ def tile_flaxattention2_s_kernel(tc, query, key, value, out):
     q_view = query.rearrange(view, t=PACK, a=DUO, pair=PAIRS, c=PASSES)
     k_view = key.rearrange(view, t=PACK, a=DUO, pair=PAIRS, c=PASSES)
     k_long_view = key.rearrange("b (j a pair) h d -> pair (b j) a (h d)", a=DUO, pair=PAIRS)
-    out_view = out.rearrange("(a pair) d e -> pair a d e", a=DUO)
+    out_view = out.rearrange("(a pair) d e -> a d pair e", a=DUO)
 
     with ExitStack() as ctx:
         ctx.enter_context(tc.manual_schedule())
@@ -186,7 +186,7 @@ def tile_flaxattention2_s_kernel(tc, query, key, value, out):
         inverse = keep.tile([P, PAIRS], F32)
         probs = keep.tile([P, PAIRS, DH], F32)
 
-        def exponentials(pair):
+        def row_minimum(pair):
             scores = score_tiles[pair]
             one = slice(pair, pair + 1)
             for a in range(DUO):
@@ -200,6 +200,9 @@ def tile_flaxattention2_s_kernel(tc, query, key, value, out):
                     op1=ALU.min,
                     accum_out=shift[half, one],
                 )
+
+        def exponentials(pair):
+            one = slice(pair, pair + 1)
             nc.scalar.activation(
                 out=grown[:, pair, :],
                 in_=flipped[:, pair, :],
@@ -209,57 +212,73 @@ def tile_flaxattention2_s_kernel(tc, query, key, value, out):
                 accum_out=row_sum[:, one],
             )
 
-        def divide_and_store(pair, queues):
-            one = slice(pair, pair + 1)
-            nc.vector.reciprocal(out=inverse[:, one], in_=row_sum[:, one])
-            nc.vector.tensor_scalar(
-                out=probs[:, pair, :],
-                in0=grown[:, pair, :],
-                scalar1=inverse[:, one],
-                scalar2=None,
-                op0=ALU.mult,
-            )
+        def invert(first):
+            some = slice(first, first + 2)
+            nc.vector.reciprocal(out=inverse[:, some], in_=row_sum[:, some])
+
+        def scale_and_store(first, queues):
+            for pair in (first + 1, first):
+                nc.vector.tensor_scalar(
+                    out=probs[:, pair, :],
+                    in0=grown[:, pair, :],
+                    scalar1=inverse[:, pair : pair + 1],
+                    scalar2=None,
+                    op0=ALU.mult,
+                )
+            some = slice(first, first + 2)
             for a, queue in enumerate(queues):
-                queue.dma_start(out=out_view[pair, a], in_=probs[a * DH : (a + 1) * DH, pair, :])
+                queue.dma_start(out=out_view[a, :, some], in_=probs[a * DH : (a + 1) * DH, some, :])
 
         transpose_first(0)
         transpose_first(1)
         copy_first(0)
         copy_first(1)
         transpose_second(0)
-        transpose_second(1)
         regroup_q(0)
         copy_second(nc.vector.tensor_copy, 0)
-        copy_second(nc.scalar.copy, 1)
-        regroup_k(1)
+        transpose_first(2)
+        transpose_second(1)
         quantise_q(0, range(PASSES))
+        copy_first(2)
+        transpose_first(3)
+        copy_second(nc.scalar.copy, 1)
+        copy_first(3)
+        regroup_q(1)
+        transpose_second(2)
         quantise_k(0)
+        copy_second(nc.vector.tensor_copy, 2)
+        transpose_first(4)
+        copy_first(4)
+        transpose_second(3)
+        transpose_first(5)
+        copy_second(nc.scalar.copy, 3)
+        copy_first(5)
+        quantise_q(1, range(PASSES))
+        regroup_q(2)
+        transpose_second(4)
+        transpose_second(5)
+        quantise_k(1)
         multiply(0, 0, True)
         multiply(0, 1, False)
-
-        quantise_k(1)
-        regroup_q(1)
-        exponentials(0)
-        quantise_q(1, range(PASSES))
         multiply(1, 0, True)
         multiply(1, 1, False)
-        regroup_k(2)
-        divide_and_store(0, (nc.sync, nc.sync))
-        quantise_k(2)
-        regroup_q(2)
-        exponentials(1)
+        copy_second(nc.vector.tensor_copy, 4)
+        copy_second(nc.scalar.copy, 5)
+
+        regroup_k(3)
         quantise_q(2, range(PASSES))
+        quantise_k(2)
         multiply(2, 0, True)
         multiply(2, 1, False)
-        regroup_k(3)
-        divide_and_store(1, (nc.sync, nc.sync))
-        quantise_k(3)
         regroup_q(3)
-        exponentials(2)
+        quantise_k(3)
         quantise_q(3, range(1, 2))
         multiply(3, 1, True)
         quantise_q(3, range(0, 1))
         multiply(3, 0, False)
-        divide_and_store(2, (nc.sync, nc.sync))
-        exponentials(3)
-        divide_and_store(3, (nc.sync, nc.scalar))
+        for pair in range(PAIRS):
+            row_minimum(pair)
+            exponentials(pair)
+        for first, queues in ((0, (nc.sync, nc.sync)), (2, (nc.sync, nc.scalar))):
+            invert(first)
+            scale_and_store(first, queues)

from contextlib import ExitStack

import concourse.mybir as mybir
from concourse.masks import make_identity

BF16 = mybir.dt.bfloat16
F32 = mybir.dt.float32
U32 = mybir.dt.uint32
U8 = mybir.dt.uint8
FP8X4 = mybir.dt.float8_e4m3fn_x4
ALU = mybir.AluOpType
ACT = mybir.ActivationFunctionType

P = 128
PACK = 4
SEQ, HEADS, DH = 1024, 8, 64
MATS = SEQ // P
QUAD = 32
QUADS = P // QUAD
PASSES = HEADS // QUADS
DUO = 2
PAIRS = MATS // DUO
LONG_PAIRS = 3
MS = P // QUADS
TPS = PACK // 2
COLS = DUO * DH
RUN = 4
SCALE = DH ** -0.5

FLOPS = 2 * MATS * DH * DH * SEQ
BYTES = 2 * SEQ * HEADS * DH * 2 + MATS * DH * DH * 4


def regroup(copy, raw, grouped, c):
    copy(
        out=grouped[:, c].rearrange("p a (e i) t -> p a e t i", i=RUN),
        in_=raw.rearrange("p (t a) (c d) -> p t a c d", a=DUO, c=PASSES)[:, :, :, c].rearrange(
            "p t a (e i) -> p a e t i", i=RUN
        ),
    )


def tile_flaxattention2_s_kernel(tc, query, key, value, out):
    nc = tc.nc
    view = "b (m t a pair) (q c) d -> pair q (b m) (t a) (c d)"
    q_view = query.rearrange(view, t=PACK, a=DUO, pair=PAIRS, c=PASSES)
    k_view = key.rearrange(view, t=PACK, a=DUO, pair=PAIRS, c=PASSES)
    k_long_view = key.rearrange("b (j a pair) h d -> pair (b j) a (h d)", a=DUO, pair=PAIRS)
    out_view = out.rearrange("(a pair) d e -> a d pair e", a=DUO)

    with ExitStack() as ctx:
        ctx.enter_context(tc.manual_schedule())
        keep = ctx.enter_context(tc.tile_pool(name="keep", bufs=1))
        operands = ctx.enter_context(tc.tile_pool(name="operands", bufs=PAIRS))
        psum = ctx.enter_context(tc.psum_pool(name="psum", bufs=2))

        k_raw_tiles = []
        q_raw_tiles = []

        def load(raw, view):
            for q in (0, 2, 1, 3):
                nc.sync.dma_start(out=raw[q * QUAD : (q + 1) * QUAD], in_=view[q])

        for pair in range(PAIRS):
            if pair < LONG_PAIRS:
                k_raw = keep.tile([P, DUO, HEADS * DH], BF16, name="k_long", bufs=LONG_PAIRS)
                nc.sync.dma_start(out=k_raw[:], in_=k_long_view[pair])
            else:
                k_raw = keep.tile([P, PACK * DUO, PASSES * DH], BF16, name="k_raw", bufs=PAIRS - LONG_PAIRS)
                load(k_raw, k_view[pair])
            k_raw_tiles.append(k_raw)
            q_raw = operands.tile([P, PACK * DUO, PASSES * DH], BF16)
            load(q_raw, q_view[pair])
            q_raw_tiles.append(q_raw)

        warm = keep.tile([P, 1], F32)
        nc.vector.memset(warm[:], 0.0)
        nc.scalar.activation(out=warm[:], in_=warm[:], func=ACT.Exp)

        ident_16 = keep.tile([P, P], BF16)
        make_identity(nc, ident_16[:])
        ident_32 = keep.tile([P, P], F32)
        make_identity(nc, ident_32[:])

        first_banks = []
        word_tiles = []
        second_banks = []
        k_grouped_tiles = []
        for pair in range(PAIRS):
            k_grouped = operands.tile([P, PASSES, DUO, DH, PACK], BF16, align_bytes=64)
            k_grouped_tiles.append(k_grouped)

        def transpose_first(step):
            pair, a = divmod(step, DUO)
            bank = psum.tile([P, QUADS, P], BF16, name="first")
            for q in range(QUADS):
                nc.tensor.transpose(bank[:, q], k_raw_tiles[pair][:, a, q * P : (q + 1) * P], ident_16[:])
            first_banks.append(bank)

        def copy_first(step):
            words = keep.tile([P, TPS, QUADS * MS], F32, name="words", bufs=LONG_PAIRS * DUO)
            nc.scalar.copy(
                out=words[:],
                in_=first_banks[step][:]
                .rearrange("p q j -> p (q j)")
                .bitcast(F32)
                .rearrange("p (y s) -> p s y", s=TPS),
            )
            word_tiles.append(words)

        def transpose_second(step):
            bank = psum.tile([P, TPS, P], F32, name="second")
            for s in range(TPS):
                nc.tensor.transpose(bank[:, s], word_tiles[step][:, s], ident_32[:])
            second_banks.append(bank)

        def copy_second(copy, step):
            pair, a = divmod(step, DUO)
            words = k_grouped_tiles[pair][:].rearrange("p c a d t -> p (c a d t)").bitcast(F32)
            copy(
                out=words.rearrange("p (c a d s) -> p c a d s", c=PASSES, a=DUO, s=TPS)[:, :, a],
                in_=second_banks[step][:].rearrange("p s (c d) -> p c d s", c=PASSES),
            )

        def regroup_both_passes(raw, grouped):
            regroup(nc.scalar.copy, raw[:], grouped, 0)
            regroup(nc.vector.tensor_copy, raw[:], grouped, 1)

        def quantise(grouped, codes, scales, first, passes):
            cols = slice(first * COLS, (first + passes) * COLS)
            nc.vector.quantize_mx(
                out=codes[:, cols].bitcast(FP8X4),
                scales=scales[:, cols],
                in_=grouped[:, first : first + passes].rearrange("p c a d t -> p (c a d t)"),
            )

        def regroup_k(pair):
            regroup_both_passes(k_raw_tiles[pair], k_grouped_tiles[pair])

        k_operands = {}

        def quantise_k(pair):
            k_codes = operands.tile([P, PASSES * COLS], U32, align_bytes=64)
            k_scales = operands.tile([P, PASSES * COLS], U8, align_bytes=64)
            quantise(k_grouped_tiles[pair], k_codes, k_scales, 0, PASSES)
            k_operands[pair] = (k_codes, k_scales)

        q_grouped_tiles = {}
        q_operands = {}

        def regroup_q(pair):
            q_grouped = operands.tile([P, PASSES, DUO, DH, PACK], BF16, align_bytes=64)
            regroup_both_passes(q_raw_tiles[pair], q_grouped)
            q_grouped_tiles[pair] = q_grouped

        def quantise_q(pair, passes):
            if pair not in q_operands:
                q_codes = operands.tile([P, PASSES * COLS], U32, align_bytes=64)
                q_scales = operands.tile([P, PASSES * COLS], U8, align_bytes=64)
                q_operands[pair] = (q_codes, q_scales)
            quantise(q_grouped_tiles[pair], *q_operands[pair], passes.start, len(passes))

        score_tiles = {}

        def multiply(pair, c, start):
            if start:
                scores = psum.tile([P, COLS], F32, bufs=PAIRS)
                score_tiles[pair] = scores
            q_codes, q_scales = q_operands[pair]
            k_codes, k_scales = k_operands[pair]
            cols = slice(c * COLS, (c + 1) * COLS)
            nc.tensor.matmul_mx(
                out=score_tiles[pair][:],
                lhsT=q_codes[:, cols].bitcast(FP8X4),
                lhsT_scale=q_scales[:, cols],
                rhs=k_codes[:, cols].bitcast(FP8X4),
                rhs_scale=k_scales[:, cols],
                start=start,
                stop=not start,
            )

        flipped = keep.tile([P, PAIRS, DH], F32)
        shift = keep.tile([P, PAIRS], F32)
        grown = keep.tile([P, PAIRS, DH], F32)
        row_sum = keep.tile([P, PAIRS], F32)
        inverse = keep.tile([P, PAIRS], F32)
        probs = keep.tile([P, PAIRS, DH], F32)

        def row_minimum(pair):
            scores = score_tiles[pair]
            one = slice(pair, pair + 1)
            for a in range(DUO):
                half = slice(a * DH, (a + 1) * DH)
                nc.vector.tensor_scalar(
                    out=flipped[half, pair, :],
                    in0=scores[half, half],
                    scalar1=-SCALE,
                    scalar2=None,
                    op0=ALU.mult,
                    op1=ALU.min,
                    accum_out=shift[half, one],
                )

        def exponentials(pair):
            one = slice(pair, pair + 1)
            nc.scalar.activation(
                out=grown[:, pair, :],
                in_=flipped[:, pair, :],
                func=ACT.Exp,
                bias=shift[:, one],
                scale=-1.0,
                accum_out=row_sum[:, one],
            )

        def invert(first):
            some = slice(first, first + 2)
            nc.vector.reciprocal(out=inverse[:, some], in_=row_sum[:, some])

        def scale_and_store(first, queues):
            for pair in (first + 1, first):
                nc.vector.tensor_scalar(
                    out=probs[:, pair, :],
                    in0=grown[:, pair, :],
                    scalar1=inverse[:, pair : pair + 1],
                    scalar2=None,
                    op0=ALU.mult,
                )
            some = slice(first, first + 2)
            for a, queue in enumerate(queues):
                queue.dma_start(out=out_view[a, :, some], in_=probs[a * DH : (a + 1) * DH, some, :])

        transpose_first(0)
        transpose_first(1)
        copy_first(0)
        copy_first(1)
        transpose_second(0)
        regroup_q(0)
        copy_second(nc.vector.tensor_copy, 0)
        transpose_first(2)
        transpose_second(1)
        quantise_q(0, range(PASSES))
        copy_first(2)
        transpose_first(3)
        copy_second(nc.scalar.copy, 1)
        copy_first(3)
        regroup_q(1)
        transpose_second(2)
        quantise_k(0)
        copy_second(nc.vector.tensor_copy, 2)
        transpose_first(4)
        copy_first(4)
        transpose_second(3)
        transpose_first(5)
        copy_second(nc.scalar.copy, 3)
        copy_first(5)
        quantise_q(1, range(PASSES))
        regroup_q(2)
        transpose_second(4)
        transpose_second(5)
        quantise_k(1)
        multiply(0, 0, True)
        multiply(0, 1, False)
        multiply(1, 0, True)
        multiply(1, 1, False)
        copy_second(nc.vector.tensor_copy, 4)
        copy_second(nc.scalar.copy, 5)

        regroup_k(3)
        quantise_q(2, range(PASSES))
        quantise_k(2)
        multiply(2, 0, True)
        multiply(2, 1, False)
        regroup_q(3)
        quantise_k(3)
        quantise_q(3, range(1, 2))
        multiply(3, 1, True)
        quantise_q(3, range(0, 1))
        multiply(3, 0, False)
        for pair in range(PAIRS):
            row_minimum(pair)
            exponentials(pair)
        for first, queues in ((0, (nc.sync, nc.sync)), (2, (nc.sync, nc.scalar))):
            invert(first)
            scale_and_store(first, queues)
